import numpy as np
import ml_dtypes


def mxq(x, axis, fmt="e4m3"):
    dtype, down = {"e4m3": (ml_dtypes.float8_e4m3fn, 7), "e5m2": (ml_dtypes.float8_e5m2, 14)}[fmt]
    v = np.moveaxis(np.asarray(x, np.float32).astype(ml_dtypes.bfloat16).astype(np.float64), axis, -1)
    blocks = v.reshape(v.shape[:-1] + (-1, 32))
    amax = np.abs(blocks).max(-1, keepdims=True)
    byte = np.maximum(np.where(amax > 0, np.frexp(amax)[1] - 1 + 127, 0) - down, 1)
    scale = np.exp2(byte - 127.0)
    codes = (blocks / scale).astype(np.float32).astype(dtype).astype(np.float64)
    return np.moveaxis((codes * scale).reshape(v.shape), -1, axis)


WIDE = False


def mx_kscale(k):
    if not WIDE:
        return np.ones(k)
    levels = np.array([10, -10, 5, -5, 0])
    a = np.random.permutation(np.resize(levels, k // 512 * 4)).reshape(k // 512, 4)
    idx = np.arange(k)
    return np.exp2(a[idx // 512, idx % 128 // 32])


BF16 = ml_dtypes.bfloat16


def bf(x):
    return np.asarray(x, np.float32).astype(BF16)


def f64(x):
    return np.asarray(x).astype(np.float64)


E2M1 = np.array([0.0, 0.5, 1.0, 1.5, 2.0, 3.0, 4.0, 6.0, -0.0, -0.5, -1.0, -1.5, -2.0, -3.0, -4.0, -6.0])


def pack_weight(w, fmt):
    k, n = w.shape
    w = f64(bf(w)).reshape(k // 32, 32, n)
    amax = np.abs(w).max(1)
    if fmt == "e4m3":
        byte = np.frexp(amax)[1] - 1 + 127 - 7
    else:
        mant, ex = np.frexp(amax / 6.0)
        byte = np.where(mant > 0.5, ex, ex - 1) + 127
    byte = np.clip(np.where(amax > 0, byte, 1), 1, 254)
    scaled = (w * np.exp2(127.0 - byte)[:, None, :]).reshape(k, n).astype(np.float32)
    by_word = np.ascontiguousarray(scaled.reshape(k // 512, 128, 4, n).transpose(0, 1, 3, 2))
    if fmt == "e4m3":
        words = by_word.astype(ml_dtypes.float8_e4m3fn).view(np.uint8)
    else:
        c = by_word.astype(ml_dtypes.float4_e2m1fn).view(np.uint8) & 0xF
        words = c[..., 0::2] | (c[..., 1::2] << 4)
    return np.ascontiguousarray(words), np.ascontiguousarray(byte.astype(np.uint8).reshape(k // 512, 16, n))


def unpack_weight(words, scales, fmt):
    g, p, n, _ = words.shape
    if fmt == "e4m3":
        vals = np.ascontiguousarray(words).view(ml_dtypes.float8_e4m3fn).astype(np.float64)
    else:
        nib = np.empty((g, p, n, 4), np.uint8)
        nib[..., 0::2] = words & 0xF
        nib[..., 1::2] = words >> 4
        vals = E2M1[nib]
    vals = vals * np.repeat(np.exp2(scales.astype(np.float64) - 127.0), 8, axis=1)[..., None]
    return vals.transpose(0, 1, 3, 2).reshape(g * 512, n)


B, C, S, OUT = 256, 4, 64, 128
IN = C * S * S
HS = S // 2
SUB, BLK = 4, 32


def haar_dwt2_features(x):
    x4 = x.reshape(x.shape[0], C, S, S)
    a = x4[:, :, 0::2, 0::2]
    bq = x4[:, :, 0::2, 1::2]
    c = x4[:, :, 1::2, 0::2]
    d = x4[:, :, 1::2, 1::2]
    LL = (a + bq + c + d) * 0.5
    LH = (a + bq - c - d) * 0.5
    HL = (a - bq + c - d) * 0.5
    HH = (a - bq - c + d) * 0.5
    t = np.stack([LL, LH, HL, HH], axis=2)
    return t.reshape(x.shape[0], -1)


def setup_inputs():
    g = mx_kscale(IN).reshape(-1, SUB, BLK)[:, 0, :].reshape(C, HS, HS)
    gx = np.repeat(np.repeat(g, 2, axis=1), 2, axis=2).reshape(IN)
    gt = np.repeat(g[:, None], SUB, axis=1).reshape(IN)
    x = bf(np.random.standard_normal((B, IN)) * gx)
    w = np.random.standard_normal((OUT, IN)) * (1.0 / np.sqrt(IN)) / gt
    words, scales = pack_weight(np.ascontiguousarray(w.T), "e4m3")
    b = bf(np.random.standard_normal(OUT) * 0.5)
    return {"x": x, "W_words": words, "W_scales": scales, "b": b}


def reference(x, W_words, W_scales, b):
    t = haar_dwt2_features(f64(x))
    return (mxq(t, 1, "e4m3") @ unpack_weight(W_words, W_scales, "e4m3")) + f64(b)

@@ -1,0 +1,146 @@
+from contextlib import ExitStack
+
+import concourse.mybir as mybir
+from concourse.masks import make_identity
+
+F32 = mybir.dt.float32
+BF16 = mybir.dt.bfloat16
+I32 = mybir.dt.int32
+U32 = mybir.dt.uint32
+U8 = mybir.dt.uint8
+FP8X4 = mybir.dt.float8_e4m3fn_x4
+ADD = mybir.AluOpType.add
+SUB = mybir.AluOpType.subtract
+MULT = mybir.AluOpType.mult
+
+P = 128
+BATCH = 256
+HALVES = BATCH // P
+CHANNELS = 4
+SIDE = 64
+FEATURES = CHANNELS * SIDE * SIDE
+OUT = 128
+PACK = 4
+K_PASS = P * PACK
+PASSES = FEATURES // K_PASS
+SUBBANDS = 4
+
+CHUNK_PIXELS = SUBBANDS * K_PASS
+CHUNKS = FEATURES // CHUNK_PIXELS
+CHUNK_WORDS = CHUNK_PIXELS // 2
+BLOCK_ROWS = 16
+WORD_GROUPS = 8
+
+FLOPS = 2 * BATCH * FEATURES * OUT
+
+
+def tile_waveletlinearlayer_kernel(tc, x, W_words, W_scales, b, out):
+    nc = tc.nc
+    with ExitStack() as ctx:
+        keep = ctx.enter_context(tc.tile_pool(name="keep", bufs=1))
+        sorted_pool = ctx.enter_context(tc.tile_pool(name="sorted", bufs=3))
+        lower_pool = ctx.enter_context(tc.tile_pool(name="lower", bufs=3))
+        stage_pool = ctx.enter_context(tc.tile_pool(name="stage", bufs=2))
+        mx_pool = ctx.enter_context(tc.tile_pool(name="mx", bufs=2))
+        turn_psum = ctx.enter_context(tc.psum_pool(name="turn", bufs=3))
+        acc_psum = ctx.enter_context(tc.psum_pool(name="acc", bufs=1))
+
+        identity = keep.tile([P, P], F32)
+        make_identity(nc, identity[:])
+
+        x_sb = keep.tile([P, CHUNKS, HALVES, CHUNK_PIXELS], BF16)
+        w_words = keep.tile([P, PASSES, OUT], U32, align_bytes=64)
+        w_scales = keep.tile([P, PASSES, OUT], U8, align_bytes=64)
+        bias = keep.tile([P, OUT], BF16)
+
+        def load_x(chunk):
+            for half in range(HALVES):
+                nc.sync.dma_start(
+                    out=x_sb[:, chunk, half, :],
+                    in_=x[half * P : (half + 1) * P, chunk * CHUNK_PIXELS : (chunk + 1) * CHUNK_PIXELS],
+                )
+
+        nc.vector.memset(w_scales[:].bitcast(I32), 0)
+        load_x(0)
+        for quadrant in range(4):
+            nc.sync.dma_start(
+                out=w_scales[32 * quadrant : 32 * quadrant + 4, :, :].bitcast(I32),
+                in_=W_scales[:, 4 * quadrant : 4 * quadrant + 4, :].rearrange("g r n -> r g n").bitcast(I32),
+            )
+        nc.sync.dma_start(out=bias[:], in_=b.partition_broadcast(P))
+        passes_per_channel = PASSES // CHANNELS
+        for chunk in range(1, CHUNKS):
+            if chunk % 2 == 1:
+                first = (chunk // 2) * passes_per_channel
+                nc.sync.dma_start(
+                    out=w_words[:, first : first + passes_per_channel, :].bitcast(I32),
+                    in_=W_words[first : first + passes_per_channel]
+                    .rearrange("g p n t -> p g (n t)")
+                    .bitcast(I32),
+                )
+            load_x(chunk)
+
+        acc = [acc_psum.tile([P, OUT], F32, name="acc%d" % half) for half in range(HALVES)]
+
+        for chunk in range(CHUNKS):
+            channel = chunk // 2
+            rows_half = chunk % 2
+            col_sum = stage_pool.tile([P, HALVES, P, PACK, 2], F32)
+            col_diff = stage_pool.tile([P, HALVES, P, PACK, 2], F32)
+            for half in range(HALVES):
+                words = x_sb[:, chunk, half, :].bitcast(F32).rearrange(
+                    "p (i r q t) -> p r i q t", i=BLOCK_ROWS, r=2, q=WORD_GROUPS, t=PACK
+                )
+                in_order = sorted_pool.tile([P, 2, PACK, P], F32)
+                for r in range(2):
+                    nc.scalar.copy(
+                        out=in_order[:, r].rearrange("p t (i q) -> p i q t", i=BLOCK_ROWS),
+                        in_=words[:, r],
+                    )
+                upper = turn_psum.tile([P, PACK, P], F32)
+                lower = turn_psum.tile([P, PACK, P], F32)
+                for t in range(PACK):
+                    nc.tensor.transpose(upper[:, t, :], in_order[:, 0, t, :], identity[:])
+                for t in range(PACK):
+                    nc.tensor.transpose(lower[:, t, :], in_order[:, 1, t, :], identity[:])
+                lower_sb = lower_pool.tile([P, P, PACK], F32)
+                nc.scalar.copy(out=lower_sb[:], in_=lower[:].rearrange("p t n -> p n t"))
+                upper_px = upper[:].bitcast(BF16).rearrange("p t (n e) -> p n t e", e=2)
+                lower_px = lower_sb[:].bitcast(BF16).rearrange("p n (t e) -> p n t e", e=2)
+                nc.vector.tensor_tensor(out=col_sum[:, half], in0=upper_px, in1=lower_px, op=ADD)
+                nc.vector.tensor_tensor(out=col_diff[:, half], in0=upper_px, in1=lower_px, op=SUB)
+
+            sums = col_sum[:].rearrange("p h n t e -> p (h n t) e")
+            diffs = col_diff[:].rearrange("p h n t e -> p (h n t) e")
+            doubled = mx_pool.tile([P, SUBBANDS, HALVES * P * PACK], BF16, align_bytes=64)
+            nc.vector.tensor_tensor(out=doubled[:, 0, :], in0=sums[:, :, 0], in1=sums[:, :, 1], op=ADD)
+            nc.vector.tensor_tensor(out=doubled[:, 1, :], in0=diffs[:, :, 0], in1=diffs[:, :, 1], op=ADD)
+            nc.vector.tensor_tensor(out=doubled[:, 2, :], in0=sums[:, :, 0], in1=sums[:, :, 1], op=SUB)
+            nc.vector.tensor_tensor(out=doubled[:, 3, :], in0=diffs[:, :, 0], in1=diffs[:, :, 1], op=SUB)
+
+            codes = mx_pool.tile([P, SUBBANDS, HALVES, P], U32, align_bytes=64)
+            scales = mx_pool.tile([P, SUBBANDS, HALVES, P], U8, align_bytes=64)
+            nc.vector.quantize_mx(
+                out=codes[:].rearrange("p s h n -> p (s h n)").bitcast(FP8X4),
+                scales=scales[:].rearrange("p s h n -> p (s h n)"),
+                in_=doubled[:].rearrange("p s c -> p (s c)"),
+            )
+            for subband in range(SUBBANDS):
+                g = (channel * SUBBANDS + subband) * 2 + rows_half
+                for half in range(HALVES):
+                    nc.tensor.matmul_mx(
+                        out=acc[half][:],
+                        lhsT=codes[:, subband, half, :].bitcast(FP8X4),
+                        lhsT_scale=scales[:, subband, half, :],
+                        rhs=w_words[:, g, :].bitcast(FP8X4),
+                        rhs_scale=w_scales[:, g, :],
+                        start=(chunk == 0 and subband == 0),
+                        stop=(chunk == CHUNKS - 1 and subband == SUBBANDS - 1),
+                    )
+
+        result = keep.tile([P, HALVES, OUT], F32)
+        for half in range(HALVES):
+            nc.vector.scalar_tensor_tensor(
+                out=result[:, half, :], in0=acc[half][:], scalar=0.5, in1=bias[:], op0=MULT, op1=ADD
+            )
+            nc.sync.dma_start(out=out[half * P : (half + 1) * P, :], in_=result[:, half, :])

@@ -11,7 +11,7 @@ U8 = mybir.dt.uint8
 FP8X4 = mybir.dt.float8_e4m3fn_x4
 ADD = mybir.AluOpType.add
 SUB = mybir.AluOpType.subtract
-MULT = mybir.AluOpType.mult
+COPY = mybir.ActivationFunctionType.Copy
 
 P = 128
 BATCH = 256
@@ -27,9 +27,10 @@ SUBBANDS = 4
 
 CHUNK_PIXELS = SUBBANDS * K_PASS
 CHUNKS = FEATURES // CHUNK_PIXELS
-CHUNK_WORDS = CHUNK_PIXELS // 2
 BLOCK_ROWS = 16
-WORD_GROUPS = 8
+GROUPS = 8
+SUM, DIFF = 0, 1
+UPPER, LOWER = 0, 1
 
 FLOPS = 2 * BATCH * FEATURES * OUT
 
@@ -38,12 +39,11 @@ def tile_waveletlinearlayer_kernel(tc, x, W_words, W_scales, b, out):
     nc = tc.nc
     with ExitStack() as ctx:
         keep = ctx.enter_context(tc.tile_pool(name="keep", bufs=1))
-        sorted_pool = ctx.enter_context(tc.tile_pool(name="sorted", bufs=3))
-        lower_pool = ctx.enter_context(tc.tile_pool(name="lower", bufs=3))
-        stage_pool = ctx.enter_context(tc.tile_pool(name="stage", bufs=2))
+        row_pool = ctx.enter_context(tc.tile_pool(name="rows", bufs=2))
         mx_pool = ctx.enter_context(tc.tile_pool(name="mx", bufs=2))
-        turn_psum = ctx.enter_context(tc.psum_pool(name="turn", bufs=3))
+        turn_psum = ctx.enter_context(tc.psum_pool(name="turn", bufs=6))
         acc_psum = ctx.enter_context(tc.psum_pool(name="acc", bufs=1))
+        ctx.enter_context(tc.manual_schedule())
 
         identity = keep.tile([P, P], F32)
         make_identity(nc, identity[:])
@@ -62,6 +62,7 @@ def tile_waveletlinearlayer_kernel(tc, x, W_words, W_scales, b, out):
 
         nc.vector.memset(w_scales[:].bitcast(I32), 0)
         load_x(0)
+        load_x(1)
         for quadrant in range(4):
             nc.sync.dma_start(
                 out=w_scales[32 * quadrant : 32 * quadrant + 4, :, :].bitcast(I32),
@@ -69,62 +70,79 @@ def tile_waveletlinearlayer_kernel(tc, x, W_words, W_scales, b, out):
             )
         nc.sync.dma_start(out=bias[:], in_=b.partition_broadcast(P))
         passes_per_channel = PASSES // CHANNELS
-        for chunk in range(1, CHUNKS):
-            if chunk % 2 == 1:
-                first = (chunk // 2) * passes_per_channel
-                nc.sync.dma_start(
-                    out=w_words[:, first : first + passes_per_channel, :].bitcast(I32),
-                    in_=W_words[first : first + passes_per_channel]
-                    .rearrange("g p n t -> p g (n t)")
-                    .bitcast(I32),
-                )
-            load_x(chunk)
+        for channel in range(CHANNELS):
+            first = channel * passes_per_channel
+            nc.sync.dma_start(
+                out=w_words[:, first : first + passes_per_channel, :].bitcast(I32),
+                in_=W_words[first : first + passes_per_channel].rearrange("g p n t -> p g (n t)").bitcast(I32),
+            )
+            if channel > 0:
+                load_x(2 * channel)
+                load_x(2 * channel + 1)
 
         acc = [acc_psum.tile([P, OUT], F32, name="acc%d" % half) for half in range(HALVES)]
 
-        for chunk in range(CHUNKS):
-            channel = chunk // 2
-            rows_half = chunk % 2
-            col_sum = stage_pool.tile([P, HALVES, P, PACK, 2], F32)
-            col_diff = stage_pool.tile([P, HALVES, P, PACK, 2], F32)
-            for half in range(HALVES):
-                words = x_sb[:, chunk, half, :].bitcast(F32).rearrange(
-                    "p (i r q t) -> p r i q t", i=BLOCK_ROWS, r=2, q=WORD_GROUPS, t=PACK
-                )
-                in_order = sorted_pool.tile([P, 2, PACK, P], F32)
-                for r in range(2):
-                    nc.scalar.copy(
-                        out=in_order[:, r].rearrange("p t (i q) -> p i q t", i=BLOCK_ROWS),
-                        in_=words[:, r],
+        def along_rows(chunk):
+            pixels = x_sb[:, chunk].rearrange(
+                "p h (i r q t e) -> p r e h i q t", i=BLOCK_ROWS, r=2, q=GROUPS, t=PACK, e=2
+            )
+            terms = row_pool.tile([P, 2, 2, HALVES, PACK, P], F32)
+            negated = row_pool.tile([P, 2, HALVES, PACK, P], F32)
+            for kind, op in ((SUM, ADD), (DIFF, SUB)):
+                for r in (LOWER, UPPER):
+                    nc.vector.tensor_tensor(
+                        out=terms[:, r, kind].rearrange("p h t (i q) -> p h i q t", i=BLOCK_ROWS),
+                        in0=pixels[:, r, 0],
+                        in1=pixels[:, r, 1],
+                        op=op,
                     )
-                upper = turn_psum.tile([P, PACK, P], F32)
-                lower = turn_psum.tile([P, PACK, P], F32)
-                for t in range(PACK):
-                    nc.tensor.transpose(upper[:, t, :], in_order[:, 0, t, :], identity[:])
-                for t in range(PACK):
-                    nc.tensor.transpose(lower[:, t, :], in_order[:, 1, t, :], identity[:])
-                lower_sb = lower_pool.tile([P, P, PACK], F32)
-                nc.scalar.copy(out=lower_sb[:], in_=lower[:].rearrange("p t n -> p n t"))
-                upper_px = upper[:].bitcast(BF16).rearrange("p t (n e) -> p n t e", e=2)
-                lower_px = lower_sb[:].bitcast(BF16).rearrange("p n (t e) -> p n t e", e=2)
-                nc.vector.tensor_tensor(out=col_sum[:, half], in0=upper_px, in1=lower_px, op=ADD)
-                nc.vector.tensor_tensor(out=col_diff[:, half], in0=upper_px, in1=lower_px, op=SUB)
+                if kind == SUM:
+                    nc.scalar.mul(out=negated[:, SUM], in_=terms[:, LOWER, SUM], mul=-1.0)
+                else:
+                    nc.vector.tensor_scalar_mul(out=negated[:, DIFF], in0=terms[:, LOWER, DIFF], scalar1=-1.0)
+            return terms, negated
 
-            sums = col_sum[:].rearrange("p h n t e -> p (h n t) e")
-            diffs = col_diff[:].rearrange("p h n t e -> p (h n t) e")
-            doubled = mx_pool.tile([P, SUBBANDS, HALVES * P * PACK], BF16, align_bytes=64)
-            nc.vector.tensor_tensor(out=doubled[:, 0, :], in0=sums[:, :, 0], in1=sums[:, :, 1], op=ADD)
-            nc.vector.tensor_tensor(out=doubled[:, 1, :], in0=diffs[:, :, 0], in1=diffs[:, :, 1], op=ADD)
-            nc.vector.tensor_tensor(out=doubled[:, 2, :], in0=sums[:, :, 0], in1=sums[:, :, 1], op=SUB)
-            nc.vector.tensor_tensor(out=doubled[:, 3, :], in0=diffs[:, :, 0], in1=diffs[:, :, 1], op=SUB)
+        def across_rows(terms, negated):
+            features = mx_pool.tile([P, SUBBANDS, HALVES, P, PACK], BF16, align_bytes=64)
+            recipe = (
+                (0, SUM, terms[:, LOWER, SUM]),
+                (2, DIFF, terms[:, LOWER, DIFF]),
+                (3, DIFF, negated[:, DIFF]),
+                (1, SUM, negated[:, SUM]),
+            )
+            for subband, kind, lower in recipe:
+                for half in range(HALVES):
+                    turned = turn_psum.tile([P, PACK, P], F32)
+                    for t in range(PACK):
+                        nc.tensor.matmul(
+                            out=turned[:, t, :], lhsT=terms[:, UPPER, kind, half, t, :], rhs=identity[:],
+                            is_transpose=True, start=True, stop=False,
+                        )
+                        nc.tensor.matmul(
+                            out=turned[:, t, :], lhsT=lower[:, half, t, :], rhs=identity[:],
+                            is_transpose=True, start=False, stop=True,
+                        )
+                    nc.scalar.activation(
+                        out=features[:, subband, half],
+                        in_=turned[:].rearrange("p t n -> p n t"),
+                        func=COPY,
+                        scale=0.5,
+                    )
+            return features
 
+        def quantise(features):
             codes = mx_pool.tile([P, SUBBANDS, HALVES, P], U32, align_bytes=64)
             scales = mx_pool.tile([P, SUBBANDS, HALVES, P], U8, align_bytes=64)
             nc.vector.quantize_mx(
                 out=codes[:].rearrange("p s h n -> p (s h n)").bitcast(FP8X4),
                 scales=scales[:].rearrange("p s h n -> p (s h n)"),
-                in_=doubled[:].rearrange("p s c -> p (s c)"),
+                in_=features[:].rearrange("p s h n t -> p (s h n t)"),
             )
+            return codes, scales
+
+        def multiply(chunk, codes, scales):
+            channel = chunk // 2
+            rows_half = chunk % 2
             for subband in range(SUBBANDS):
                 g = (channel * SUBBANDS + subband) * 2 + rows_half
                 for half in range(HALVES):
@@ -138,9 +156,17 @@ def tile_waveletlinearlayer_kernel(tc, x, W_words, W_scales, b, out):
                         stop=(chunk == CHUNKS - 1 and subband == SUBBANDS - 1),
                     )
 
+        features = None
+        for chunk in range(CHUNKS + 1):
+            earlier = features
+            if chunk < CHUNKS:
+                terms, negated = along_rows(chunk)
+                features = across_rows(terms, negated)
+            if chunk > 0:
+                codes, scales = quantise(earlier)
+                multiply(chunk - 1, codes, scales)
+
         result = keep.tile([P, HALVES, OUT], F32)
         for half in range(HALVES):
-            nc.vector.scalar_tensor_tensor(
-                out=result[:, half, :], in0=acc[half][:], scalar=0.5, in1=bias[:], op0=MULT, op1=ADD
-            )
+            nc.vector.tensor_tensor(out=result[:, half, :], in0=acc[half][:], in1=bias[:], op=ADD)
             nc.sync.dma_start(out=out[half * P : (half + 1) * P, :], in_=result[:, half, :])

@@ -105,12 +105,12 @@ def tile_waveletlinearlayer_kernel(tc, x, W_words, W_scales, b, out):
         def across_rows(terms, negated):
             features = mx_pool.tile([P, SUBBANDS, HALVES, P, PACK], BF16, align_bytes=64)
             recipe = (
-                (0, SUM, terms[:, LOWER, SUM]),
-                (2, DIFF, terms[:, LOWER, DIFF]),
-                (3, DIFF, negated[:, DIFF]),
-                (1, SUM, negated[:, SUM]),
+                (SUM, terms[:, LOWER, SUM]),
+                (SUM, negated[:, SUM]),
+                (DIFF, terms[:, LOWER, DIFF]),
+                (DIFF, negated[:, DIFF]),
             )
-            for subband, kind, lower in recipe:
+            for subband, (kind, lower) in enumerate(recipe):
                 for half in range(HALVES):
                     turned = turn_psum.tile([P, PACK, P], F32)
                     for t in range(PACK):
@@ -133,11 +133,12 @@ def tile_waveletlinearlayer_kernel(tc, x, W_words, W_scales, b, out):
         def quantise(features):
             codes = mx_pool.tile([P, SUBBANDS, HALVES, P], U32, align_bytes=64)
             scales = mx_pool.tile([P, SUBBANDS, HALVES, P], U8, align_bytes=64)
-            nc.vector.quantize_mx(
-                out=codes[:].rearrange("p s h n -> p (s h n)").bitcast(FP8X4),
-                scales=scales[:].rearrange("p s h n -> p (s h n)"),
-                in_=features[:].rearrange("p s h n t -> p (s h n t)"),
-            )
+            for subband in range(SUBBANDS):
+                nc.vector.quantize_mx(
+                    out=codes[:, subband].rearrange("p h n -> p (h n)").bitcast(FP8X4),
+                    scales=scales[:, subband].rearrange("p h n -> p (h n)"),
+                    in_=features[:, subband].rearrange("p h n t -> p (h n t)"),
+                )
             return codes, scales
 
         def multiply(chunk, codes, scales):

@@ -99,7 +99,7 @@ def tile_waveletlinearlayer_kernel(tc, x, W_words, W_scales, b, out):
                 if kind == SUM:
                     nc.scalar.mul(out=negated[:, SUM], in_=terms[:, LOWER, SUM], mul=-1.0)
                 else:
-                    nc.vector.tensor_scalar_mul(out=negated[:, DIFF], in0=terms[:, LOWER, DIFF], scalar1=-1.0)
+                    nc.vector.tensor_scalar_mul(out=negated[:, DIFF, 0], in0=terms[:, LOWER, DIFF, 0], scalar1=-1.0)
             return terms, negated
 
         def across_rows(terms, negated):
@@ -111,6 +111,8 @@ def tile_waveletlinearlayer_kernel(tc, x, W_words, W_scales, b, out):
                 (DIFF, negated[:, DIFF]),
             )
             for subband, (kind, lower) in enumerate(recipe):
+                if subband == 1:
+                    nc.scalar.mul(out=negated[:, DIFF, 1], in_=terms[:, LOWER, DIFF, 1], mul=-1.0)
                 for half in range(HALVES):
                     turned = turn_psum.tile([P, PACK, P], F32)
                     for t in range(PACK):

@@ -33,6 +33,7 @@ SUM, DIFF = 0, 1
 UPPER, LOWER = 0, 1
 
 FLOPS = 2 * BATCH * FEATURES * OUT
+WARM_UP = 6
 
 
 def tile_waveletlinearlayer_kernel(tc, x, W_words, W_scales, b, out):
@@ -81,6 +82,13 @@ def tile_waveletlinearlayer_kernel(tc, x, W_words, W_scales, b, out):
                 load_x(2 * channel + 1)
 
         acc = [acc_psum.tile([P, OUT], F32, name="acc%d" % half) for half in range(HALVES)]
+
+        warm = turn_psum.tile([P, PACK, P], F32, name="turned")
+        for repeat in range(WARM_UP):
+            nc.tensor.matmul(
+                out=warm[:].rearrange("p t n -> p (t n)"), lhsT=x_sb[:, 0, 0, 0:P], rhs=x_sb[:, 0, 0, 0 : PACK * P],
+                start=True, stop=True,
+            )
 
         def along_rows(chunk):
             pixels = x_sb[:, chunk].rearrange(

@@ -33,7 +33,7 @@ SUM, DIFF = 0, 1
 UPPER, LOWER = 0, 1
 
 FLOPS = 2 * BATCH * FEATURES * OUT
-WARM_UP = 6
+WARM_UP = 4
 
 
 def tile_waveletlinearlayer_kernel(tc, x, W_words, W_scales, b, out):
@@ -56,10 +56,12 @@ def tile_waveletlinearlayer_kernel(tc, x, W_words, W_scales, b, out):
 
         def load_x(chunk):
             for half in range(HALVES):
-                nc.sync.dma_start(
-                    out=x_sb[:, chunk, half, :],
-                    in_=x[half * P : (half + 1) * P, chunk * CHUNK_PIXELS : (chunk + 1) * CHUNK_PIXELS],
-                )
+                cuts = (0, PACK * P, CHUNK_PIXELS) if (chunk == 0 and half == 0) else (0, CHUNK_PIXELS)
+                for first, last in zip(cuts[:-1], cuts[1:]):
+                    nc.sync.dma_start(
+                        out=x_sb[:, chunk, half, first:last],
+                        in_=x[half * P : (half + 1) * P, chunk * CHUNK_PIXELS + first : chunk * CHUNK_PIXELS + last],
+                    )
 
         nc.vector.memset(w_scales[:].bitcast(I32), 0)
         load_x(0)
@@ -90,64 +92,59 @@ def tile_waveletlinearlayer_kernel(tc, x, W_words, W_scales, b, out):
                 start=True, stop=True,
             )
 
-        def along_rows(chunk):
+        def new_rows():
+            terms = row_pool.tile([P, 2, 2, HALVES, PACK, P], F32, name="terms")
+            negated = row_pool.tile([P, 2, HALVES, PACK, P], F32, name="negated")
+            features = mx_pool.tile([P, SUBBANDS, HALVES, P, PACK], BF16, align_bytes=64, name="features")
+            return terms, negated, features
+
+        def along_rows(chunk, terms, kind, halves):
             pixels = x_sb[:, chunk].rearrange(
                 "p h (i r q t e) -> p r e h i q t", i=BLOCK_ROWS, r=2, q=GROUPS, t=PACK, e=2
             )
-            terms = row_pool.tile([P, 2, 2, HALVES, PACK, P], F32)
-            negated = row_pool.tile([P, 2, HALVES, PACK, P], F32)
-            for kind, op in ((SUM, ADD), (DIFF, SUB)):
-                for r in (LOWER, UPPER):
-                    nc.vector.tensor_tensor(
-                        out=terms[:, r, kind].rearrange("p h t (i q) -> p h i q t", i=BLOCK_ROWS),
-                        in0=pixels[:, r, 0],
-                        in1=pixels[:, r, 1],
-                        op=op,
-                    )
-                if kind == SUM:
-                    nc.scalar.mul(out=negated[:, SUM], in_=terms[:, LOWER, SUM], mul=-1.0)
-                else:
-                    nc.vector.tensor_scalar_mul(out=negated[:, DIFF, 0], in0=terms[:, LOWER, DIFF, 0], scalar1=-1.0)
-            return terms, negated
+            for r in (LOWER, UPPER):
+                nc.vector.tensor_tensor(
+                    out=terms[:, r, kind, halves].rearrange("p h t (i q) -> p h i q t", i=BLOCK_ROWS),
+                    in0=pixels[:, r, 0, halves],
+                    in1=pixels[:, r, 1, halves],
+                    op=(ADD if kind == SUM else SUB),
+                )
 
-        def across_rows(terms, negated):
-            features = mx_pool.tile([P, SUBBANDS, HALVES, P, PACK], BF16, align_bytes=64)
-            recipe = (
-                (SUM, terms[:, LOWER, SUM]),
-                (SUM, negated[:, SUM]),
-                (DIFF, terms[:, LOWER, DIFF]),
-                (DIFF, negated[:, DIFF]),
+        def negate(on_vector, terms, negated, kind, halves):
+            if on_vector:
+                nc.vector.tensor_scalar_mul(out=negated[:, kind, halves], in0=terms[:, LOWER, kind, halves], scalar1=-1.0)
+            else:
+                nc.scalar.mul(out=negated[:, kind, halves], in_=terms[:, LOWER, kind, halves], mul=-1.0)
+
+        def across_rows(terms, negated, features, subband, half):
+            kind = (SUM, SUM, DIFF, DIFF)[subband]
+            lower = (terms[:, LOWER, SUM], negated[:, SUM], terms[:, LOWER, DIFF], negated[:, DIFF])[subband]
+            turned = turn_psum.tile([P, PACK, P], F32, name="turned")
+            for t in range(PACK):
+                nc.tensor.matmul(
+                    out=turned[:, t, :], lhsT=terms[:, UPPER, kind, half, t, :], rhs=identity[:],
+                    is_transpose=True, start=True, stop=False,
+                )
+                nc.tensor.matmul(
+                    out=turned[:, t, :], lhsT=lower[:, half, t, :], rhs=identity[:],
+                    is_transpose=True, start=False, stop=True,
+                )
+            nc.scalar.activation(
+                out=features[:, subband, half],
+                in_=turned[:].rearrange("p t n -> p n t"),
+                func=COPY,
+                scale=0.5,
             )
-            for subband, (kind, lower) in enumerate(recipe):
-                if subband == 1:
-                    nc.scalar.mul(out=negated[:, DIFF, 1], in_=terms[:, LOWER, DIFF, 1], mul=-1.0)
-                for half in range(HALVES):
-                    turned = turn_psum.tile([P, PACK, P], F32)
-                    for t in range(PACK):
-                        nc.tensor.matmul(
-                            out=turned[:, t, :], lhsT=terms[:, UPPER, kind, half, t, :], rhs=identity[:],
-                            is_transpose=True, start=True, stop=False,
-                        )
-                        nc.tensor.matmul(
-                            out=turned[:, t, :], lhsT=lower[:, half, t, :], rhs=identity[:],
-                            is_transpose=True, start=False, stop=True,
-                        )
-                    nc.scalar.activation(
-                        out=features[:, subband, half],
-                        in_=turned[:].rearrange("p t n -> p n t"),
-                        func=COPY,
-                        scale=0.5,
-                    )
-            return features
 
-        def quantise(features):
+        def quantise(features, calls):
             codes = mx_pool.tile([P, SUBBANDS, HALVES, P], U32, align_bytes=64)
             scales = mx_pool.tile([P, SUBBANDS, HALVES, P], U8, align_bytes=64)
-            for subband in range(SUBBANDS):
+            width = SUBBANDS // calls
+            for first in range(0, SUBBANDS, width):
                 nc.vector.quantize_mx(
-                    out=codes[:, subband].rearrange("p h n -> p (h n)").bitcast(FP8X4),
-                    scales=scales[:, subband].rearrange("p h n -> p (h n)"),
-                    in_=features[:, subband].rearrange("p h n t -> p (h n t)"),
+                    out=codes[:, first : first + width].rearrange("p s h n -> p (s h n)").bitcast(FP8X4),
+                    scales=scales[:, first : first + width].rearrange("p s h n -> p (s h n)"),
+                    in_=features[:, first : first + width].rearrange("p s h n t -> p (s h n t)"),
                 )
             return codes, scales
 
@@ -167,14 +164,42 @@ def tile_waveletlinearlayer_kernel(tc, x, W_words, W_scales, b, out):
                         stop=(chunk == CHUNKS - 1 and subband == SUBBANDS - 1),
                     )
 
+        BOTH = slice(0, HALVES)
         features = None
         for chunk in range(CHUNKS + 1):
             earlier = features
-            if chunk < CHUNKS:
-                terms, negated = along_rows(chunk)
-                features = across_rows(terms, negated)
+            if chunk == 0:
+                terms, negated, features = new_rows()
+                for half in range(HALVES):
+                    one = slice(half, half + 1)
+                    along_rows(chunk, terms, SUM, one)
+                    along_rows(chunk, terms, DIFF, one)
+                    if half == 0:
+                        negate(True, terms, negated, DIFF, one)
+                negate(False, terms, negated, SUM, slice(0, 1))
+                across_rows(terms, negated, features, 0, 0)
+                across_rows(terms, negated, features, 1, 0)
+                across_rows(terms, negated, features, 2, 0)
+                negate(False, terms, negated, SUM, slice(1, 2))
+                across_rows(terms, negated, features, 3, 0)
+                across_rows(terms, negated, features, 0, 1)
+                negate(False, terms, negated, DIFF, slice(1, 2))
+                across_rows(terms, negated, features, 1, 1)
+                across_rows(terms, negated, features, 2, 1)
+                across_rows(terms, negated, features, 3, 1)
+            elif chunk < CHUNKS:
+                terms, negated, features = new_rows()
+                along_rows(chunk, terms, SUM, BOTH)
+                negate(False, terms, negated, SUM, BOTH)
+                along_rows(chunk, terms, DIFF, BOTH)
+                negate(True, terms, negated, DIFF, slice(0, 1))
+                for subband in range(SUBBANDS):
+                    if subband == 1:
+                        negate(False, terms, negated, DIFF, slice(1, 2))
+                    for half in range(HALVES):
+                        across_rows(terms, negated, features, subband, half)
             if chunk > 0:
-                codes, scales = quantise(earlier)
+                codes, scales = quantise(earlier, SUBBANDS if chunk == CHUNKS else 1)
                 multiply(chunk - 1, codes, scales)
 
         result = keep.tile([P, HALVES, OUT], F32)

@@ -148,25 +148,30 @@ def tile_waveletlinearlayer_kernel(tc, x, W_words, W_scales, b, out):
                 )
             return codes, scales
 
+        def multiply_one(total, codes, scales, chunk, subband, start, stop):
+            g = (chunk // 2 * SUBBANDS + subband) * 2 + chunk % 2
+            nc.tensor.matmul_mx(
+                out=total,
+                lhsT=codes.bitcast(FP8X4),
+                lhsT_scale=scales,
+                rhs=w_words[:, g, :].bitcast(FP8X4),
+                rhs_scale=w_scales[:, g, :],
+                start=start,
+                stop=stop,
+            )
+
         def multiply(chunk, codes, scales):
-            channel = chunk // 2
-            rows_half = chunk % 2
             for subband in range(SUBBANDS):
-                g = (channel * SUBBANDS + subband) * 2 + rows_half
                 for half in range(HALVES):
-                    nc.tensor.matmul_mx(
-                        out=acc[half][:],
-                        lhsT=codes[:, subband, half, :].bitcast(FP8X4),
-                        lhsT_scale=scales[:, subband, half, :],
-                        rhs=w_words[:, g, :].bitcast(FP8X4),
-                        rhs_scale=w_scales[:, g, :],
+                    multiply_one(
+                        acc[half][:], codes[:, subband, half, :], scales[:, subband, half, :], chunk, subband,
                         start=(chunk == 0 and subband == 0),
-                        stop=(chunk == CHUNKS - 1 and subband == SUBBANDS - 1),
+                        stop=False,
                     )
 
         BOTH = slice(0, HALVES)
         features = None
-        for chunk in range(CHUNKS + 1):
+        for chunk in range(CHUNKS - 1):
             earlier = features
             if chunk == 0:
                 terms, negated, features = new_rows()
@@ -187,7 +192,7 @@ def tile_waveletlinearlayer_kernel(tc, x, W_words, W_scales, b, out):
                 across_rows(terms, negated, features, 1, 1)
                 across_rows(terms, negated, features, 2, 1)
                 across_rows(terms, negated, features, 3, 1)
-            elif chunk < CHUNKS:
+            elif chunk < CHUNKS - 1:
                 terms, negated, features = new_rows()
                 along_rows(chunk, terms, SUM, BOTH)
                 negate(False, terms, negated, SUM, BOTH)
@@ -199,10 +204,64 @@ def tile_waveletlinearlayer_kernel(tc, x, W_words, W_scales, b, out):
                     for half in range(HALVES):
                         across_rows(terms, negated, features, subband, half)
             if chunk > 0:
-                codes, scales = quantise(earlier, SUBBANDS if chunk == CHUNKS else 1)
+                codes, scales = quantise(earlier, 1)
                 multiply(chunk - 1, codes, scales)
 
+        last = CHUNKS - 1
+        earlier = features
+        terms = row_pool.tile([P, 2, 2, HALVES, PACK, P], F32, name="terms")
+        negated = row_pool.tile([P, 2, HALVES, PACK, P], F32, name="negated")
+        features = mx_pool.tile([P, SUBBANDS, HALVES, P, PACK], BF16, align_bytes=64, name="features")
+        row_terms = keep.tile([P, HALVES, CHUNK_PIXELS // 2], F32)
+        paired = keep.tile([P, 2, 2, HALVES, P, 2], BF16, align_bytes=64)
+        along_rows(last, terms, SUM, BOTH)
+        for half in range(HALVES):
+            negate(False, terms, negated, SUM, slice(half, half + 1))
+        pixels = x_sb[:, last].rearrange("p h (k e) -> p e h k", e=2)
+        nc.vector.tensor_tensor(out=row_terms[:], in0=pixels[:, 0], in1=pixels[:, 1], op=SUB)
+        rows = row_terms[:].rearrange("p h (i r q u e) -> p r h i q u e", i=BLOCK_ROWS, r=2, q=GROUPS, u=2, e=2)
+        for s in range(2):
+            nc.vector.tensor_tensor(
+                out=paired[:, s].rearrange("p u h (i q) e -> p h i q u e", i=BLOCK_ROWS),
+                in0=rows[:, UPPER],
+                in1=rows[:, LOWER],
+                op=(ADD, SUB)[s],
+            )
+        for subband in range(2):
+            for half in range(HALVES):
+                across_rows(terms, negated, features, subband, half)
+        for s in range(2):
+            turned = turn_psum.tile([P, PACK, P], F32, name="turned")
+            for half in range(HALVES):
+                for u in range(2):
+                    nc.tensor.matmul(
+                        out=turned[:, 2 * half + u, :],
+                        lhsT=paired[:, s, u, half].rearrange("p m e -> p (m e)").bitcast(F32),
+                        rhs=identity[:],
+                        is_transpose=True, start=True, stop=True,
+                    )
+            nc.scalar.copy(
+                out=features[:].bitcast(F32)[:, 2 + s],
+                in_=turned[:].rearrange("p (h u) n -> p h n u", h=HALVES),
+            )
+        codes, scales = quantise(earlier, 1)
+        multiply(last - 1, codes, scales)
+        codes, scales = quantise(features, SUBBANDS)
+        doubled = [turn_psum.tile([P, PACK, P], F32, name="turned") for half in range(HALVES)]
+        for subband in range(SUBBANDS):
+            for half in range(HALVES):
+                multiply_one(
+                    acc[half][:] if subband < 2 else doubled[half][:, 0, :],
+                    codes[:, subband, half, :], scales[:, subband, half, :], last, subband,
+                    start=(subband == 2), stop=(subband % 2 == 1),
+                )
         result = keep.tile([P, HALVES, OUT], F32)
+        final = keep.tile([P, HALVES, OUT], F32)
         for half in range(HALVES):
             nc.vector.tensor_tensor(out=result[:, half, :], in0=acc[half][:], in1=bias[:], op=ADD)
-            nc.sync.dma_start(out=out[half * P : (half + 1) * P, :], in_=result[:, half, :])
+        for half in range(HALVES):
+            nc.vector.scalar_tensor_tensor(
+                out=final[:, half, :], in0=doubled[half][:, 0, :], scalar=0.5, in1=result[:, half, :],
+                op0=mybir.AluOpType.mult, op1=ADD,
+            )
+            nc.sync.dma_start(out=out[half * P : (half + 1) * P, :], in_=final[:, half, :])

@@ -33,7 +33,9 @@ SUM, DIFF = 0, 1
 UPPER, LOWER = 0, 1
 
 FLOPS = 2 * BATCH * FEATURES * OUT
-WARM_UP = 4
+WARM_UP = 2
+PIECES = 4
+PIECE_ROWS = BLOCK_ROWS // PIECES
 
 
 def tile_waveletlinearlayer_kernel(tc, x, W_words, W_scales, b, out):
@@ -46,17 +48,36 @@ def tile_waveletlinearlayer_kernel(tc, x, W_words, W_scales, b, out):
         acc_psum = ctx.enter_context(tc.psum_pool(name="acc", bufs=1))
         ctx.enter_context(tc.manual_schedule())
 
+        zeros = keep.tile([P, PACK * P], BF16)
+        nc.gpsimd.memset(zeros[:], 0.0)
+        identity16 = keep.tile([P, P], BF16)
+        make_identity(nc, identity16[:])
+        haar = keep.tile([P, SUBBANDS, P // SUBBANDS], BF16)
+        along = keep.tile([P, 2, 2, P // SUBBANDS], BF16)
+        unit = identity16[:].rearrange("p (i r q e) -> p e r i q", i=PIECE_ROWS, r=2, q=GROUPS, e=2)
+        for kind in (SUM, DIFF):
+            nc.gpsimd.tensor_tensor(
+                out=along[:, kind].rearrange("p r (i q) -> p r i q", i=PIECE_ROWS),
+                in0=unit[:, 0], in1=unit[:, 1], op=(ADD if kind == SUM else SUB),
+            )
+        for subband in range(SUBBANDS):
+            kind = (SUM, SUM, DIFF, DIFF)[subband]
+            nc.gpsimd.tensor_tensor(
+                out=haar[:, subband], in0=along[:, kind, UPPER], in1=along[:, kind, LOWER],
+                op=(ADD, SUB, ADD, SUB)[subband],
+            )
         identity = keep.tile([P, P], F32)
         make_identity(nc, identity[:])
 
         x_sb = keep.tile([P, CHUNKS, HALVES, CHUNK_PIXELS], BF16)
         w_words = keep.tile([P, PASSES, OUT], U32, align_bytes=64)
-        w_scales = keep.tile([P, PASSES, OUT], U8, align_bytes=64)
+        w_scales = keep.tile([P, PASSES + PIECES, OUT], U8, align_bytes=64)
+        piece_words = keep.tile([P, PIECES, OUT], U32, align_bytes=64)
         bias = keep.tile([P, OUT], BF16)
 
         def load_x(chunk):
             for half in range(HALVES):
-                cuts = (0, PACK * P, CHUNK_PIXELS) if (chunk == 0 and half == 0) else (0, CHUNK_PIXELS)
+                cuts = range(0, CHUNK_PIXELS + 1, K_PASS) if (chunk == 0 and half == 0) else (0, CHUNK_PIXELS)
                 for first, last in zip(cuts[:-1], cuts[1:]):
                     nc.sync.dma_start(
                         out=x_sb[:, chunk, half, first:last],
@@ -66,12 +87,22 @@ def tile_waveletlinearlayer_kernel(tc, x, W_words, W_scales, b, out):
         nc.vector.memset(w_scales[:].bitcast(I32), 0)
         load_x(0)
         load_x(1)
+        load_x(2)
         for quadrant in range(4):
             nc.sync.dma_start(
-                out=w_scales[32 * quadrant : 32 * quadrant + 4, :, :].bitcast(I32),
+                out=w_scales[32 * quadrant : 32 * quadrant + 4, 0:PASSES, :].bitcast(I32),
                 in_=W_scales[:, 4 * quadrant : 4 * quadrant + 4, :].rearrange("g r n -> r g n").bitcast(I32),
             )
-        nc.sync.dma_start(out=bias[:], in_=b.partition_broadcast(P))
+        for subband in range(SUBBANDS):
+            nc.sync.dma_start(
+                out=w_scales[32 * subband : 32 * subband + 4, PASSES : PASSES + PIECES, :].bitcast(I32),
+                in_=W_scales[2 * subband].rearrange("(g i) n -> i g n", g=PIECES).bitcast(I32),
+            )
+        for subband in range(SUBBANDS):
+            nc.sync.dma_start(
+                out=piece_words[32 * subband : 32 * subband + 32].bitcast(I32),
+                in_=W_words[2 * subband].rearrange("(g p) n t -> p g (n t)", g=PIECES).bitcast(I32),
+            )
         passes_per_channel = PASSES // CHANNELS
         for channel in range(CHANNELS):
             first = channel * passes_per_channel
@@ -79,16 +110,16 @@ def tile_waveletlinearlayer_kernel(tc, x, W_words, W_scales, b, out):
                 out=w_words[:, first : first + passes_per_channel, :].bitcast(I32),
                 in_=W_words[first : first + passes_per_channel].rearrange("g p n t -> p g (n t)").bitcast(I32),
             )
-            if channel > 0:
-                load_x(2 * channel)
-                load_x(2 * channel + 1)
+            for chunk in range(2 * channel + 3, min(2 * channel + 5, CHUNKS)):
+                load_x(chunk)
+        nc.sync.dma_start(out=bias[:], in_=b.partition_broadcast(P))
 
         acc = [acc_psum.tile([P, OUT], F32, name="acc%d" % half) for half in range(HALVES)]
 
         warm = turn_psum.tile([P, PACK, P], F32, name="turned")
         for repeat in range(WARM_UP):
             nc.tensor.matmul(
-                out=warm[:].rearrange("p t n -> p (t n)"), lhsT=x_sb[:, 0, 0, 0:P], rhs=x_sb[:, 0, 0, 0 : PACK * P],
+                out=warm[:].rearrange("p t n -> p (t n)"), lhsT=zeros[:, 0:P], rhs=zeros[:],
                 start=True, stop=True,
             )
 
@@ -148,14 +179,14 @@ def tile_waveletlinearlayer_kernel(tc, x, W_words, W_scales, b, out):
                 )
             return codes, scales
 
-        def multiply_one(total, codes, scales, chunk, subband, start, stop):
+        def multiply_one(total, codes, scales, chunk, subband, start, stop, piece=None):
             g = (chunk // 2 * SUBBANDS + subband) * 2 + chunk % 2
             nc.tensor.matmul_mx(
                 out=total,
                 lhsT=codes.bitcast(FP8X4),
                 lhsT_scale=scales,
-                rhs=w_words[:, g, :].bitcast(FP8X4),
-                rhs_scale=w_scales[:, g, :],
+                rhs=(w_words[:, g, :] if piece is None else piece_words[:, piece, :]).bitcast(FP8X4),
+                rhs_scale=w_scales[:, g if piece is None else PASSES + piece, :],
                 start=start,
                 stop=stop,
             )
@@ -167,6 +198,7 @@ def tile_waveletlinearlayer_kernel(tc, x, W_words, W_scales, b, out):
                         acc[half][:], codes[:, subband, half, :], scales[:, subband, half, :], chunk, subband,
                         start=(chunk == 0 and subband == 0),
                         stop=False,
+                        piece=(subband if chunk == 0 and half == 0 else None),
                     )
 
         BOTH = slice(0, HALVES)
@@ -175,23 +207,47 @@ def tile_waveletlinearlayer_kernel(tc, x, W_words, W_scales, b, out):
             earlier = features
             if chunk == 0:
                 terms, negated, features = new_rows()
-                for half in range(HALVES):
-                    one = slice(half, half + 1)
-                    along_rows(chunk, terms, SUM, one)
-                    along_rows(chunk, terms, DIFF, one)
-                    if half == 0:
-                        negate(True, terms, negated, DIFF, one)
-                negate(False, terms, negated, SUM, slice(0, 1))
-                across_rows(terms, negated, features, 0, 0)
-                across_rows(terms, negated, features, 1, 0)
-                across_rows(terms, negated, features, 2, 0)
-                negate(False, terms, negated, SUM, slice(1, 2))
-                across_rows(terms, negated, features, 3, 0)
-                across_rows(terms, negated, features, 0, 1)
-                negate(False, terms, negated, DIFF, slice(1, 2))
-                across_rows(terms, negated, features, 1, 1)
-                across_rows(terms, negated, features, 2, 1)
-                across_rows(terms, negated, features, 3, 1)
+                sorted_pairs = keep.tile([P, PIECES, PACK, K_PASS // 8], F32)
+                pixels_up = keep.tile([P, PIECES, PACK * P], BF16)
+
+                def sort_piece(g):
+                    nc.vector.tensor_copy(
+                        out=sorted_pairs[:, g].rearrange("p t m -> p m t"),
+                        in_=x_sb[:, 0, 0, g * K_PASS : (g + 1) * K_PASS].bitcast(F32).rearrange("p (m t) -> p m t", t=PACK),
+                    )
+
+                def turn_piece(g):
+                    turned = turn_psum.tile([P, PACK, P], BF16, name="turned")
+                    for t in range(PACK):
+                        nc.tensor.transpose(turned[:, t, :], sorted_pairs[:, g, t].bitcast(BF16), identity16[:])
+                    copy = nc.vector.tensor_copy if g < 2 else nc.scalar.copy
+                    copy(out=pixels_up[:, g], in_=turned[:].rearrange("p t n -> p (t n)"))
+
+                def transform_piece(g):
+                    made = turn_psum.tile([P, PACK, P], F32, name="turned")
+                    nc.tensor.matmul(
+                        out=made[:].rearrange("p t n -> p (t n)"), lhsT=haar[:].rearrange("p s m -> p (s m)"),
+                        rhs=pixels_up[:, g], start=True, stop=True,
+                    )
+                    nc.scalar.activation(
+                        out=features[:, g, 0], in_=made[:].rearrange("p t n -> p n t"), func=COPY, scale=0.5
+                    )
+
+                for g in range(PIECES):
+                    sort_piece(g)
+                turn_piece(0)
+                turn_piece(1)
+                for g in range(PIECES):
+                    transform_piece(g)
+                    if g + 2 < PIECES:
+                        turn_piece(g + 2)
+                one = slice(1, 2)
+                along_rows(chunk, terms, SUM, one)
+                negate(True, terms, negated, SUM, one)
+                along_rows(chunk, terms, DIFF, one)
+                negate(True, terms, negated, DIFF, one)
+                for subband in range(SUBBANDS):
+                    across_rows(terms, negated, features, subband, 1)
             elif chunk < CHUNKS - 1:
                 terms, negated, features = new_rows()
                 along_rows(chunk, terms, SUM, BOTH)

@@ -33,7 +33,7 @@ SUM, DIFF = 0, 1
 UPPER, LOWER = 0, 1
 
 FLOPS = 2 * BATCH * FEATURES * OUT
-WARM_UP = 2
+WARM_UP = 4
 PIECES = 4
 PIECE_ROWS = BLOCK_ROWS // PIECES
 
@@ -48,8 +48,8 @@ def tile_waveletlinearlayer_kernel(tc, x, W_words, W_scales, b, out):
         acc_psum = ctx.enter_context(tc.psum_pool(name="acc", bufs=1))
         ctx.enter_context(tc.manual_schedule())
 
-        zeros = keep.tile([P, PACK * P], BF16)
-        nc.gpsimd.memset(zeros[:], 0.0)
+        identity = keep.tile([P, P], F32)
+        make_identity(nc, identity[:])
         identity16 = keep.tile([P, P], BF16)
         make_identity(nc, identity16[:])
         haar = keep.tile([P, SUBBANDS, P // SUBBANDS], BF16)
@@ -66,8 +66,6 @@ def tile_waveletlinearlayer_kernel(tc, x, W_words, W_scales, b, out):
                 out=haar[:, subband], in0=along[:, kind, UPPER], in1=along[:, kind, LOWER],
                 op=(ADD, SUB, ADD, SUB)[subband],
             )
-        identity = keep.tile([P, P], F32)
-        make_identity(nc, identity[:])
 
         x_sb = keep.tile([P, CHUNKS, HALVES, CHUNK_PIXELS], BF16)
         w_words = keep.tile([P, PASSES, OUT], U32, align_bytes=64)
@@ -116,12 +114,24 @@ def tile_waveletlinearlayer_kernel(tc, x, W_words, W_scales, b, out):
 
         acc = [acc_psum.tile([P, OUT], F32, name="acc%d" % half) for half in range(HALVES)]
 
-        warm = turn_psum.tile([P, PACK, P], F32, name="turned")
-        for repeat in range(WARM_UP):
-            nc.tensor.matmul(
-                out=warm[:].rearrange("p t n -> p (t n)"), lhsT=zeros[:, 0:P], rhs=zeros[:],
-                start=True, stop=True,
-            )
+        def raise_clock(count):
+            idle = turn_psum.tile([P, PACK, P], F32, name="turned")
+            for repeat in range(count):
+                nc.tensor.matmul(out=idle[:, 0, :], lhsT=identity[:], rhs=identity[:], start=True, stop=True)
+
+        def hold_clock(count):
+            idle = turn_psum.tile([P, PACK, P], F32, name="turned")
+            for repeat in range(count):
+                nc.tensor.matmul_mx(
+                    out=idle[:].rearrange("p t n -> p (t n)"),
+                    lhsT=w_words[:, 0, :].bitcast(FP8X4),
+                    lhsT_scale=w_scales[:, 0, :],
+                    rhs=w_words[:, 4:8, :].rearrange("p g n -> p (g n)").bitcast(FP8X4),
+                    rhs_scale=w_scales[:, 4:8, :].rearrange("p g n -> p (g n)"),
+                    start=True, stop=True,
+                )
+
+        raise_clock(WARM_UP)
 
         def new_rows():
             terms = row_pool.tile([P, 2, 2, HALVES, PACK, P], F32, name="terms")
@@ -154,11 +164,12 @@ def tile_waveletlinearlayer_kernel(tc, x, W_words, W_scales, b, out):
             for t in range(PACK):
                 nc.tensor.matmul(
                     out=turned[:, t, :], lhsT=terms[:, UPPER, kind, half, t, :], rhs=identity[:],
-                    is_transpose=True, start=True, stop=False,
+                    is_transpose=True, start=(t == 0), stop=False,
                 )
+            for t in range(PACK):
                 nc.tensor.matmul(
                     out=turned[:, t, :], lhsT=lower[:, half, t, :], rhs=identity[:],
-                    is_transpose=True, start=False, stop=True,
+                    is_transpose=True, start=False, stop=(t == PACK - 1),
                 )
             nc.scalar.activation(
                 out=features[:, subband, half],
@@ -235,12 +246,10 @@ def tile_waveletlinearlayer_kernel(tc, x, W_words, W_scales, b, out):
 
                 for g in range(PIECES):
                     sort_piece(g)
-                turn_piece(0)
-                turn_piece(1)
+                for g in range(PIECES):
+                    turn_piece(g)
                 for g in range(PIECES):
                     transform_piece(g)
-                    if g + 2 < PIECES:
-                        turn_piece(g + 2)
                 one = slice(1, 2)
                 along_rows(chunk, terms, SUM, one)
                 negate(True, terms, negated, SUM, one)
@@ -248,6 +257,7 @@ def tile_waveletlinearlayer_kernel(tc, x, W_words, W_scales, b, out):
                 negate(True, terms, negated, DIFF, one)
                 for subband in range(SUBBANDS):
                     across_rows(terms, negated, features, subband, 1)
+                raise_clock(2)
             elif chunk < CHUNKS - 1:
                 terms, negated, features = new_rows()
                 along_rows(chunk, terms, SUM, BOTH)
@@ -259,9 +269,14 @@ def tile_waveletlinearlayer_kernel(tc, x, W_words, W_scales, b, out):
                         negate(False, terms, negated, DIFF, slice(1, 2))
                     for half in range(HALVES):
                         across_rows(terms, negated, features, subband, half)
-            if chunk > 0:
+                    if chunk == 1 and subband == 1:
+                        codes, scales = quantise(earlier, 1)
+                        multiply(0, codes, scales)
+                        hold_clock(2)
+            if chunk > 1:
                 codes, scales = quantise(earlier, 1)
                 multiply(chunk - 1, codes, scales)
+                hold_clock(2)
 
         last = CHUNKS - 1
         earlier = features

@@ -269,14 +269,14 @@ def tile_waveletlinearlayer_kernel(tc, x, W_words, W_scales, b, out):
                         negate(False, terms, negated, DIFF, slice(1, 2))
                     for half in range(HALVES):
                         across_rows(terms, negated, features, subband, half)
-                    if chunk == 1 and subband == 1:
+                    if chunk == 1 and subband == 2:
                         codes, scales = quantise(earlier, 1)
                         multiply(0, codes, scales)
-                        hold_clock(2)
+                        hold_clock(1)
             if chunk > 1:
                 codes, scales = quantise(earlier, 1)
                 multiply(chunk - 1, codes, scales)
-                hold_clock(2)
+                hold_clock(1)
 
         last = CHUNKS - 1
         earlier = features

@@ -33,6 +33,8 @@ SUM, DIFF = 0, 1
 UPPER, LOWER = 0, 1
 
 FLOPS = 2 * BATCH * FEATURES * OUT
+HALF_PIXELS = CHUNK_PIXELS // 2
+SPLIT_CHUNKS = (5, 6)
 WARM_UP = 4
 PIECES = 4
 PIECE_ROWS = BLOCK_ROWS // PIECES
@@ -75,6 +77,15 @@ def tile_waveletlinearlayer_kernel(tc, x, W_words, W_scales, b, out):
 
         def load_x(chunk):
             for half in range(HALVES):
+                if chunk in SPLIT_CHUNKS:
+                    pixels = x[half * P : (half + 1) * P, chunk * CHUNK_PIXELS : (chunk + 1) * CHUNK_PIXELS]
+                    pixels = pixels.rearrange("p (i r c) -> p r i c", r=2, c=SIDE)
+                    for r in range(2):
+                        nc.sync.dma_start(
+                            out=x_sb[:, chunk, half, r * HALF_PIXELS : (r + 1) * HALF_PIXELS].rearrange("p (i c) -> p i c", c=SIDE),
+                            in_=pixels[:, r],
+                        )
+                    continue
                 cuts = range(0, CHUNK_PIXELS + 1, K_PASS) if (chunk == 0 and half == 0) else (0, CHUNK_PIXELS)
                 for first, last in zip(cuts[:-1], cuts[1:]):
                     nc.sync.dma_start(
@@ -140,6 +151,19 @@ def tile_waveletlinearlayer_kernel(tc, x, W_words, W_scales, b, out):
             return terms, negated, features
 
         def along_rows(chunk, terms, kind, halves):
+            if chunk in SPLIT_CHUNKS:
+                split = x_sb[:, chunk].rearrange(
+                    "p h (r u v t e) -> p r e h u t v", r=2, u=BLOCK_ROWS * GROUPS // 2, v=2, t=PACK, e=2
+                )
+                for r in (LOWER, UPPER):
+                    for half in range(HALVES):
+                        nc.vector.tensor_tensor(
+                            out=terms[:, r, kind, half].rearrange("p t (u v) -> p u t v", v=2),
+                            in0=split[:, r, 0, half],
+                            in1=split[:, r, 1, half],
+                            op=(ADD if kind == SUM else SUB),
+                        )
+                return
             pixels = x_sb[:, chunk].rearrange(
                 "p h (i r q t e) -> p r e h i q t", i=BLOCK_ROWS, r=2, q=GROUPS, t=PACK, e=2
             )
@@ -214,6 +238,14 @@ def tile_waveletlinearlayer_kernel(tc, x, W_words, W_scales, b, out):
 
         BOTH = slice(0, HALVES)
         features = None
+
+        def prepare_sums(chunk):
+            tiles = new_rows()
+            terms, negated, features = tiles
+            along_rows(chunk, terms, SUM, BOTH)
+            negate(False, terms, negated, SUM, BOTH)
+            return tiles
+
         for chunk in range(CHUNKS - 1):
             earlier = features
             if chunk == 0:
@@ -256,38 +288,34 @@ def tile_waveletlinearlayer_kernel(tc, x, W_words, W_scales, b, out):
                 along_rows(chunk, terms, DIFF, one)
                 negate(True, terms, negated, DIFF, one)
                 for subband in range(SUBBANDS):
+                    if subband == SUBBANDS - 1:
+                        following = prepare_sums(1)
                     across_rows(terms, negated, features, subband, 1)
                 raise_clock(2)
             elif chunk < CHUNKS - 1:
-                terms, negated, features = new_rows()
-                along_rows(chunk, terms, SUM, BOTH)
-                negate(False, terms, negated, SUM, BOTH)
+                terms, negated, features = following
                 along_rows(chunk, terms, DIFF, BOTH)
                 negate(True, terms, negated, DIFF, slice(0, 1))
                 for subband in range(SUBBANDS):
                     if subband == 1:
                         negate(False, terms, negated, DIFF, slice(1, 2))
+                    if subband == SUBBANDS - 1:
+                        codes, scales = quantise(earlier, 1)
+                        following = prepare_sums(chunk + 1)
+                        if chunk == 1:
+                            multiply(0, codes, scales)
+                            hold_clock(1)
                     for half in range(HALVES):
                         across_rows(terms, negated, features, subband, half)
-                    if chunk == 1 and subband == 2:
-                        codes, scales = quantise(earlier, 1)
-                        multiply(0, codes, scales)
-                        hold_clock(1)
             if chunk > 1:
-                codes, scales = quantise(earlier, 1)
                 multiply(chunk - 1, codes, scales)
                 hold_clock(1)
 
         last = CHUNKS - 1
         earlier = features
-        terms = row_pool.tile([P, 2, 2, HALVES, PACK, P], F32, name="terms")
-        negated = row_pool.tile([P, 2, HALVES, PACK, P], F32, name="negated")
-        features = mx_pool.tile([P, SUBBANDS, HALVES, P, PACK], BF16, align_bytes=64, name="features")
+        terms, negated, features = following
         row_terms = keep.tile([P, HALVES, CHUNK_PIXELS // 2], F32)
         paired = keep.tile([P, 2, 2, HALVES, P, 2], BF16, align_bytes=64)
-        along_rows(last, terms, SUM, BOTH)
-        for half in range(HALVES):
-            negate(False, terms, negated, SUM, slice(half, half + 1))
         pixels = x_sb[:, last].rearrange("p h (k e) -> p e h k", e=2)
         nc.vector.tensor_tensor(out=row_terms[:], in0=pixels[:, 0], in1=pixels[:, 1], op=SUB)
         rows = row_terms[:].rearrange("p h (i r q u e) -> p r h i q u e", i=BLOCK_ROWS, r=2, q=GROUPS, u=2, e=2)

@@ -34,7 +34,7 @@ UPPER, LOWER = 0, 1
 
 FLOPS = 2 * BATCH * FEATURES * OUT
 HALF_PIXELS = CHUNK_PIXELS // 2
-SPLIT_CHUNKS = (5, 6)
+SPLIT_CHUNKS = (4, 5, 6)
 WARM_UP = 4
 PIECES = 4
 PIECE_ROWS = BLOCK_ROWS // PIECES
@@ -82,7 +82,7 @@ def tile_waveletlinearlayer_kernel(tc, x, W_words, W_scales, b, out):
                     pixels = pixels.rearrange("p (i r c) -> p r i c", r=2, c=SIDE)
                     for r in range(2):
                         nc.sync.dma_start(
-                            out=x_sb[:, chunk, half, r * HALF_PIXELS : (r + 1) * HALF_PIXELS].rearrange("p (i c) -> p i c", c=SIDE),
+                            out=x_sb[:, chunk, r, half * HALF_PIXELS : (half + 1) * HALF_PIXELS].rearrange("p (i c) -> p i c", c=SIDE),
                             in_=pixels[:, r],
                         )
                     continue
@@ -134,42 +134,39 @@ def tile_waveletlinearlayer_kernel(tc, x, W_words, W_scales, b, out):
             idle = turn_psum.tile([P, PACK, P], F32, name="turned")
             for repeat in range(count):
                 nc.tensor.matmul_mx(
-                    out=idle[:].rearrange("p t n -> p (t n)"),
+                    out=idle[:, 0:2].rearrange("p t n -> p (t n)"),
                     lhsT=w_words[:, 0, :].bitcast(FP8X4),
                     lhsT_scale=w_scales[:, 0, :],
-                    rhs=w_words[:, 4:8, :].rearrange("p g n -> p (g n)").bitcast(FP8X4),
-                    rhs_scale=w_scales[:, 4:8, :].rearrange("p g n -> p (g n)"),
+                    rhs=w_words[:, 4:6, :].rearrange("p g n -> p (g n)").bitcast(FP8X4),
+                    rhs_scale=w_scales[:, 4:6, :].rearrange("p g n -> p (g n)"),
                     start=True, stop=True,
                 )
 
         raise_clock(WARM_UP)
 
         def new_rows():
-            terms = row_pool.tile([P, 2, 2, HALVES, PACK, P], F32, name="terms")
-            negated = row_pool.tile([P, 2, HALVES, PACK, P], F32, name="negated")
+            terms = row_pool.tile([P, 2, 2, PACK, HALVES, P], F32, name="terms")
+            negated = row_pool.tile([P, 2, PACK, HALVES, P], F32, name="negated")
             features = mx_pool.tile([P, SUBBANDS, HALVES, P, PACK], BF16, align_bytes=64, name="features")
             return terms, negated, features
 
         def along_rows(chunk, terms, kind, halves):
             if chunk in SPLIT_CHUNKS:
-                split = x_sb[:, chunk].rearrange(
-                    "p h (r u v t e) -> p r e h u t v", r=2, u=BLOCK_ROWS * GROUPS // 2, v=2, t=PACK, e=2
-                )
+                split = x_sb[:, chunk].rearrange("p r (u v t e) -> p r e u t v", v=2, t=PACK, e=2)
                 for r in (LOWER, UPPER):
-                    for half in range(HALVES):
-                        nc.vector.tensor_tensor(
-                            out=terms[:, r, kind, half].rearrange("p t (u v) -> p u t v", v=2),
-                            in0=split[:, r, 0, half],
-                            in1=split[:, r, 1, half],
-                            op=(ADD if kind == SUM else SUB),
-                        )
+                    nc.vector.tensor_tensor(
+                        out=terms[:, r, kind].rearrange("p t h (u v) -> p (h u) t v", v=2),
+                        in0=split[:, r, 0],
+                        in1=split[:, r, 1],
+                        op=(ADD if kind == SUM else SUB),
+                    )
                 return
             pixels = x_sb[:, chunk].rearrange(
                 "p h (i r q t e) -> p r e h i q t", i=BLOCK_ROWS, r=2, q=GROUPS, t=PACK, e=2
             )
             for r in (LOWER, UPPER):
                 nc.vector.tensor_tensor(
-                    out=terms[:, r, kind, halves].rearrange("p h t (i q) -> p h i q t", i=BLOCK_ROWS),
+                    out=terms[:, r, kind, :, halves].rearrange("p t h (i q) -> p h i q t", i=BLOCK_ROWS),
                     in0=pixels[:, r, 0, halves],
                     in1=pixels[:, r, 1, halves],
                     op=(ADD if kind == SUM else SUB),
@@ -177,9 +174,9 @@ def tile_waveletlinearlayer_kernel(tc, x, W_words, W_scales, b, out):
 
         def negate(on_vector, terms, negated, kind, halves):
             if on_vector:
-                nc.vector.tensor_scalar_mul(out=negated[:, kind, halves], in0=terms[:, LOWER, kind, halves], scalar1=-1.0)
+                nc.vector.tensor_scalar_mul(out=negated[:, kind, :, halves], in0=terms[:, LOWER, kind, :, halves], scalar1=-1.0)
             else:
-                nc.scalar.mul(out=negated[:, kind, halves], in_=terms[:, LOWER, kind, halves], mul=-1.0)
+                nc.scalar.mul(out=negated[:, kind, :, halves], in_=terms[:, LOWER, kind, :, halves], mul=-1.0)
 
         def across_rows(terms, negated, features, subband, half):
             kind = (SUM, SUM, DIFF, DIFF)[subband]
@@ -187,12 +184,12 @@ def tile_waveletlinearlayer_kernel(tc, x, W_words, W_scales, b, out):
             turned = turn_psum.tile([P, PACK, P], F32, name="turned")
             for t in range(PACK):
                 nc.tensor.matmul(
-                    out=turned[:, t, :], lhsT=terms[:, UPPER, kind, half, t, :], rhs=identity[:],
+                    out=turned[:, t, :], lhsT=terms[:, UPPER, kind, t, half, :], rhs=identity[:],
                     is_transpose=True, start=(t == 0), stop=False,
                 )
             for t in range(PACK):
                 nc.tensor.matmul(
-                    out=turned[:, t, :], lhsT=lower[:, half, t, :], rhs=identity[:],
+                    out=turned[:, t, :], lhsT=lower[:, t, half, :], rhs=identity[:],
                     is_transpose=True, start=False, stop=(t == PACK - 1),
                 )
             nc.scalar.activation(

@@ -306,7 +306,6 @@ def tile_waveletlinearlayer_kernel(tc, x, W_words, W_scales, b, out):
                         across_rows(terms, negated, features, subband, half)
             if chunk > 1:
                 multiply(chunk - 1, codes, scales)
-                hold_clock(1)
 
         last = CHUNKS - 1
         earlier = features

from contextlib import ExitStack

import concourse.mybir as mybir
from concourse.masks import make_identity

F32 = mybir.dt.float32
BF16 = mybir.dt.bfloat16
I32 = mybir.dt.int32
U32 = mybir.dt.uint32
U8 = mybir.dt.uint8
FP8X4 = mybir.dt.float8_e4m3fn_x4
ADD = mybir.AluOpType.add
SUB = mybir.AluOpType.subtract
COPY = mybir.ActivationFunctionType.Copy

P = 128
BATCH = 256
HALVES = BATCH // P
CHANNELS = 4
SIDE = 64
FEATURES = CHANNELS * SIDE * SIDE
OUT = 128
PACK = 4
K_PASS = P * PACK
PASSES = FEATURES // K_PASS
SUBBANDS = 4

CHUNK_PIXELS = SUBBANDS * K_PASS
CHUNKS = FEATURES // CHUNK_PIXELS
BLOCK_ROWS = 16
GROUPS = 8
SUM, DIFF = 0, 1
UPPER, LOWER = 0, 1

FLOPS = 2 * BATCH * FEATURES * OUT
HALF_PIXELS = CHUNK_PIXELS // 2
SPLIT_CHUNKS = (4, 5, 6)
WARM_UP = 4
PIECES = 4
PIECE_ROWS = BLOCK_ROWS // PIECES


def tile_waveletlinearlayer_kernel(tc, x, W_words, W_scales, b, out):
    nc = tc.nc
    with ExitStack() as ctx:
        keep = ctx.enter_context(tc.tile_pool(name="keep", bufs=1))
        row_pool = ctx.enter_context(tc.tile_pool(name="rows", bufs=2))
        mx_pool = ctx.enter_context(tc.tile_pool(name="mx", bufs=2))
        turn_psum = ctx.enter_context(tc.psum_pool(name="turn", bufs=6))
        acc_psum = ctx.enter_context(tc.psum_pool(name="acc", bufs=1))
        ctx.enter_context(tc.manual_schedule())

        identity = keep.tile([P, P], F32)
        make_identity(nc, identity[:])
        identity16 = keep.tile([P, P], BF16)
        make_identity(nc, identity16[:])
        haar = keep.tile([P, SUBBANDS, P // SUBBANDS], BF16)
        along = keep.tile([P, 2, 2, P // SUBBANDS], BF16)
        unit = identity16[:].rearrange("p (i r q e) -> p e r i q", i=PIECE_ROWS, r=2, q=GROUPS, e=2)
        for kind in (SUM, DIFF):
            nc.gpsimd.tensor_tensor(
                out=along[:, kind].rearrange("p r (i q) -> p r i q", i=PIECE_ROWS),
                in0=unit[:, 0], in1=unit[:, 1], op=(ADD if kind == SUM else SUB),
            )
        for subband in range(SUBBANDS):
            kind = (SUM, SUM, DIFF, DIFF)[subband]
            nc.gpsimd.tensor_tensor(
                out=haar[:, subband], in0=along[:, kind, UPPER], in1=along[:, kind, LOWER],
                op=(ADD, SUB, ADD, SUB)[subband],
            )

        x_sb = keep.tile([P, CHUNKS, HALVES, CHUNK_PIXELS], BF16)
        w_words = keep.tile([P, PASSES, OUT], U32, align_bytes=64)
        w_scales = keep.tile([P, PASSES + PIECES, OUT], U8, align_bytes=64)
        piece_words = keep.tile([P, PIECES, OUT], U32, align_bytes=64)
        bias = keep.tile([P, OUT], BF16)

        def load_x(chunk):
            for half in range(HALVES):
                if chunk in SPLIT_CHUNKS:
                    pixels = x[half * P : (half + 1) * P, chunk * CHUNK_PIXELS : (chunk + 1) * CHUNK_PIXELS]
                    pixels = pixels.rearrange("p (i r c) -> p r i c", r=2, c=SIDE)
                    for r in range(2):
                        nc.sync.dma_start(
                            out=x_sb[:, chunk, r, half * HALF_PIXELS : (half + 1) * HALF_PIXELS].rearrange("p (i c) -> p i c", c=SIDE),
                            in_=pixels[:, r],
                        )
                    continue
                cuts = range(0, CHUNK_PIXELS + 1, K_PASS) if (chunk == 0 and half == 0) else (0, CHUNK_PIXELS)
                for first, last in zip(cuts[:-1], cuts[1:]):
                    nc.sync.dma_start(
                        out=x_sb[:, chunk, half, first:last],
                        in_=x[half * P : (half + 1) * P, chunk * CHUNK_PIXELS + first : chunk * CHUNK_PIXELS + last],
                    )

        nc.vector.memset(w_scales[:].bitcast(I32), 0)
        load_x(0)
        load_x(1)
        load_x(2)
        for quadrant in range(4):
            nc.sync.dma_start(
                out=w_scales[32 * quadrant : 32 * quadrant + 4, 0:PASSES, :].bitcast(I32),
                in_=W_scales[:, 4 * quadrant : 4 * quadrant + 4, :].rearrange("g r n -> r g n").bitcast(I32),
            )
        for subband in range(SUBBANDS):
            nc.sync.dma_start(
                out=w_scales[32 * subband : 32 * subband + 4, PASSES : PASSES + PIECES, :].bitcast(I32),
                in_=W_scales[2 * subband].rearrange("(g i) n -> i g n", g=PIECES).bitcast(I32),
            )
        for subband in range(SUBBANDS):
            nc.sync.dma_start(
                out=piece_words[32 * subband : 32 * subband + 32].bitcast(I32),
                in_=W_words[2 * subband].rearrange("(g p) n t -> p g (n t)", g=PIECES).bitcast(I32),
            )
        passes_per_channel = PASSES // CHANNELS
        for channel in range(CHANNELS):
            first = channel * passes_per_channel
            nc.sync.dma_start(
                out=w_words[:, first : first + passes_per_channel, :].bitcast(I32),
                in_=W_words[first : first + passes_per_channel].rearrange("g p n t -> p g (n t)").bitcast(I32),
            )
            for chunk in range(2 * channel + 3, min(2 * channel + 5, CHUNKS)):
                load_x(chunk)
        nc.sync.dma_start(out=bias[:], in_=b.partition_broadcast(P))

        acc = [acc_psum.tile([P, OUT], F32, name="acc%d" % half) for half in range(HALVES)]

        def raise_clock(count):
            idle = turn_psum.tile([P, PACK, P], F32, name="turned")
            for repeat in range(count):
                nc.tensor.matmul(out=idle[:, 0, :], lhsT=identity[:], rhs=identity[:], start=True, stop=True)

        def hold_clock(count):
            idle = turn_psum.tile([P, PACK, P], F32, name="turned")
            for repeat in range(count):
                nc.tensor.matmul_mx(
                    out=idle[:, 0:2].rearrange("p t n -> p (t n)"),
                    lhsT=w_words[:, 0, :].bitcast(FP8X4),
                    lhsT_scale=w_scales[:, 0, :],
                    rhs=w_words[:, 4:6, :].rearrange("p g n -> p (g n)").bitcast(FP8X4),
                    rhs_scale=w_scales[:, 4:6, :].rearrange("p g n -> p (g n)"),
                    start=True, stop=True,
                )

        raise_clock(WARM_UP)

        def new_rows():
            terms = row_pool.tile([P, 2, 2, PACK, HALVES, P], F32, name="terms")
            negated = row_pool.tile([P, 2, PACK, HALVES, P], F32, name="negated")
            features = mx_pool.tile([P, SUBBANDS, HALVES, P, PACK], BF16, align_bytes=64, name="features")
            return terms, negated, features

        def along_rows(chunk, terms, kind, halves):
            if chunk in SPLIT_CHUNKS:
                split = x_sb[:, chunk].rearrange("p r (u v t e) -> p r e u t v", v=2, t=PACK, e=2)
                for r in (LOWER, UPPER):
                    nc.vector.tensor_tensor(
                        out=terms[:, r, kind].rearrange("p t h (u v) -> p (h u) t v", v=2),
                        in0=split[:, r, 0],
                        in1=split[:, r, 1],
                        op=(ADD if kind == SUM else SUB),
                    )
                return
            pixels = x_sb[:, chunk].rearrange(
                "p h (i r q t e) -> p r e h i q t", i=BLOCK_ROWS, r=2, q=GROUPS, t=PACK, e=2
            )
            for r in (LOWER, UPPER):
                nc.vector.tensor_tensor(
                    out=terms[:, r, kind, :, halves].rearrange("p t h (i q) -> p h i q t", i=BLOCK_ROWS),
                    in0=pixels[:, r, 0, halves],
                    in1=pixels[:, r, 1, halves],
                    op=(ADD if kind == SUM else SUB),
                )

        def negate(on_vector, terms, negated, kind, halves):
            if on_vector:
                nc.vector.tensor_scalar_mul(out=negated[:, kind, :, halves], in0=terms[:, LOWER, kind, :, halves], scalar1=-1.0)
            else:
                nc.scalar.mul(out=negated[:, kind, :, halves], in_=terms[:, LOWER, kind, :, halves], mul=-1.0)

        def across_rows(terms, negated, features, subband, half):
            kind = (SUM, SUM, DIFF, DIFF)[subband]
            lower = (terms[:, LOWER, SUM], negated[:, SUM], terms[:, LOWER, DIFF], negated[:, DIFF])[subband]
            turned = turn_psum.tile([P, PACK, P], F32, name="turned")
            for t in range(PACK):
                nc.tensor.matmul(
                    out=turned[:, t, :], lhsT=terms[:, UPPER, kind, t, half, :], rhs=identity[:],
                    is_transpose=True, start=(t == 0), stop=False,
                )
            for t in range(PACK):
                nc.tensor.matmul(
                    out=turned[:, t, :], lhsT=lower[:, t, half, :], rhs=identity[:],
                    is_transpose=True, start=False, stop=(t == PACK - 1),
                )
            nc.scalar.activation(
                out=features[:, subband, half],
                in_=turned[:].rearrange("p t n -> p n t"),
                func=COPY,
                scale=0.5,
            )

        def quantise(features, calls):
            codes = mx_pool.tile([P, SUBBANDS, HALVES, P], U32, align_bytes=64)
            scales = mx_pool.tile([P, SUBBANDS, HALVES, P], U8, align_bytes=64)
            width = SUBBANDS // calls
            for first in range(0, SUBBANDS, width):
                nc.vector.quantize_mx(
                    out=codes[:, first : first + width].rearrange("p s h n -> p (s h n)").bitcast(FP8X4),
                    scales=scales[:, first : first + width].rearrange("p s h n -> p (s h n)"),
                    in_=features[:, first : first + width].rearrange("p s h n t -> p (s h n t)"),
                )
            return codes, scales

        def multiply_one(total, codes, scales, chunk, subband, start, stop, piece=None):
            g = (chunk // 2 * SUBBANDS + subband) * 2 + chunk % 2
            nc.tensor.matmul_mx(
                out=total,
                lhsT=codes.bitcast(FP8X4),
                lhsT_scale=scales,
                rhs=(w_words[:, g, :] if piece is None else piece_words[:, piece, :]).bitcast(FP8X4),
                rhs_scale=w_scales[:, g if piece is None else PASSES + piece, :],
                start=start,
                stop=stop,
            )

        def multiply(chunk, codes, scales):
            for subband in range(SUBBANDS):
                for half in range(HALVES):
                    multiply_one(
                        acc[half][:], codes[:, subband, half, :], scales[:, subband, half, :], chunk, subband,
                        start=(chunk == 0 and subband == 0),
                        stop=False,
                        piece=(subband if chunk == 0 and half == 0 else None),
                    )

        BOTH = slice(0, HALVES)
        features = None

        def prepare_sums(chunk):
            tiles = new_rows()
            terms, negated, features = tiles
            along_rows(chunk, terms, SUM, BOTH)
            negate(False, terms, negated, SUM, BOTH)
            return tiles

        for chunk in range(CHUNKS - 1):
            earlier = features
            if chunk == 0:
                terms, negated, features = new_rows()
                sorted_pairs = keep.tile([P, PIECES, PACK, K_PASS // 8], F32)
                pixels_up = keep.tile([P, PIECES, PACK * P], BF16)

                def sort_piece(g):
                    nc.vector.tensor_copy(
                        out=sorted_pairs[:, g].rearrange("p t m -> p m t"),
                        in_=x_sb[:, 0, 0, g * K_PASS : (g + 1) * K_PASS].bitcast(F32).rearrange("p (m t) -> p m t", t=PACK),
                    )

                def turn_piece(g):
                    turned = turn_psum.tile([P, PACK, P], BF16, name="turned")
                    for t in range(PACK):
                        nc.tensor.transpose(turned[:, t, :], sorted_pairs[:, g, t].bitcast(BF16), identity16[:])
                    copy = nc.vector.tensor_copy if g < 2 else nc.scalar.copy
                    copy(out=pixels_up[:, g], in_=turned[:].rearrange("p t n -> p (t n)"))

                def transform_piece(g):
                    made = turn_psum.tile([P, PACK, P], F32, name="turned")
                    nc.tensor.matmul(
                        out=made[:].rearrange("p t n -> p (t n)"), lhsT=haar[:].rearrange("p s m -> p (s m)"),
                        rhs=pixels_up[:, g], start=True, stop=True,
                    )
                    nc.scalar.activation(
                        out=features[:, g, 0], in_=made[:].rearrange("p t n -> p n t"), func=COPY, scale=0.5
                    )

                for g in range(PIECES):
                    sort_piece(g)
                for g in range(PIECES):
                    turn_piece(g)
                for g in range(PIECES):
                    transform_piece(g)
                one = slice(1, 2)
                along_rows(chunk, terms, SUM, one)
                negate(True, terms, negated, SUM, one)
                along_rows(chunk, terms, DIFF, one)
                negate(True, terms, negated, DIFF, one)
                for subband in range(SUBBANDS):
                    if subband == SUBBANDS - 1:
                        following = prepare_sums(1)
                    across_rows(terms, negated, features, subband, 1)
                raise_clock(2)
            elif chunk < CHUNKS - 1:
                terms, negated, features = following
                along_rows(chunk, terms, DIFF, BOTH)
                negate(True, terms, negated, DIFF, slice(0, 1))
                for subband in range(SUBBANDS):
                    if subband == 1:
                        negate(False, terms, negated, DIFF, slice(1, 2))
                    if subband == SUBBANDS - 1:
                        codes, scales = quantise(earlier, 1)
                        following = prepare_sums(chunk + 1)
                        if chunk == 1:
                            multiply(0, codes, scales)
                            hold_clock(1)
                    for half in range(HALVES):
                        across_rows(terms, negated, features, subband, half)
            if chunk > 1:
                multiply(chunk - 1, codes, scales)

        last = CHUNKS - 1
        earlier = features
        terms, negated, features = following
        row_terms = keep.tile([P, HALVES, CHUNK_PIXELS // 2], F32)
        paired = keep.tile([P, 2, 2, HALVES, P, 2], BF16, align_bytes=64)
        pixels = x_sb[:, last].rearrange("p h (k e) -> p e h k", e=2)
        nc.vector.tensor_tensor(out=row_terms[:], in0=pixels[:, 0], in1=pixels[:, 1], op=SUB)
        rows = row_terms[:].rearrange("p h (i r q u e) -> p r h i q u e", i=BLOCK_ROWS, r=2, q=GROUPS, u=2, e=2)
        for s in range(2):
            nc.vector.tensor_tensor(
                out=paired[:, s].rearrange("p u h (i q) e -> p h i q u e", i=BLOCK_ROWS),
                in0=rows[:, UPPER],
                in1=rows[:, LOWER],
                op=(ADD, SUB)[s],
            )
        for subband in range(2):
            for half in range(HALVES):
                across_rows(terms, negated, features, subband, half)
        for s in range(2):
            turned = turn_psum.tile([P, PACK, P], F32, name="turned")
            for half in range(HALVES):
                for u in range(2):
                    nc.tensor.matmul(
                        out=turned[:, 2 * half + u, :],
                        lhsT=paired[:, s, u, half].rearrange("p m e -> p (m e)").bitcast(F32),
                        rhs=identity[:],
                        is_transpose=True, start=True, stop=True,
                    )
            nc.scalar.copy(
                out=features[:].bitcast(F32)[:, 2 + s],
                in_=turned[:].rearrange("p (h u) n -> p h n u", h=HALVES),
            )
        codes, scales = quantise(earlier, 1)
        multiply(last - 1, codes, scales)
        codes, scales = quantise(features, SUBBANDS)
        doubled = [turn_psum.tile([P, PACK, P], F32, name="turned") for half in range(HALVES)]
        for subband in range(SUBBANDS):
            for half in range(HALVES):
                multiply_one(
                    acc[half][:] if subband < 2 else doubled[half][:, 0, :],
                    codes[:, subband, half, :], scales[:, subband, half, :], last, subband,
                    start=(subband == 2), stop=(subband % 2 == 1),
                )
        result = keep.tile([P, HALVES, OUT], F32)
        final = keep.tile([P, HALVES, OUT], F32)
        for half in range(HALVES):
            nc.vector.tensor_tensor(out=result[:, half, :], in0=acc[half][:], in1=bias[:], op=ADD)
        for half in range(HALVES):
            nc.vector.scalar_tensor_tensor(
                out=final[:, half, :], in0=doubled[half][:, 0, :], scalar=0.5, in1=result[:, half, :],
                op0=mybir.AluOpType.mult, op1=ADD,
            )
            nc.sync.dma_start(out=out[half * P : (half + 1) * P, :], in_=final[:, half, :])
